import numpy as np
import ml_dtypes


def mxq(x, axis, fmt="e4m3"):
    dtype, down = {"e4m3": (ml_dtypes.float8_e4m3fn, 7), "e5m2": (ml_dtypes.float8_e5m2, 14)}[fmt]
    v = np.moveaxis(np.asarray(x, np.float32).astype(ml_dtypes.bfloat16).astype(np.float64), axis, -1)
    blocks = v.reshape(v.shape[:-1] + (-1, 32))
    amax = np.abs(blocks).max(-1, keepdims=True)
    byte = np.maximum(np.where(amax > 0, np.frexp(amax)[1] - 1 + 127, 0) - down, 1)
    scale = np.exp2(byte - 127.0)
    codes = (blocks / scale).astype(np.float32).astype(dtype).astype(np.float64)
    return np.moveaxis((codes * scale).reshape(v.shape), -1, axis)


WIDE = False


def mx_kscale(k):
    if not WIDE:
        return np.ones(k)
    levels = np.array([10, -10, 5, -5, 0])
    a = np.random.permutation(np.resize(levels, k // 512 * 4)).reshape(k // 512, 4)
    idx = np.arange(k)
    return np.exp2(a[idx // 512, idx % 128 // 32])


BF16 = ml_dtypes.bfloat16


def bf(x):
    return np.asarray(x, np.float32).astype(BF16)


def f64(x):
    return np.asarray(x).astype(np.float64)


B, HD, NH, H, W, F = 2, 1024, 8, 16, 32, 2048
HEAD = HD // NH
P = H * W


def rms_in(x, w, eps=1e-8):
    std = np.std(x, axis=(-2, -1), keepdims=True, ddof=1)
    return x / (std + eps) * w[None, :, None, None]


def ln(x, w, b, eps=1e-5):
    mu = np.mean(x, axis=-1, keepdims=True)
    var = np.var(x, axis=-1, keepdims=True)
    return (x - mu) / np.sqrt(var + eps) * w + b


def setup_inputs():
    n = np.random.standard_normal
    s = mx_kscale(HD)
    return {"x": bf(n((B, HD, H, W)) * (0.5 + np.random.random((B, HD, 1, 1))) + 0.5 * n((B, HD, 1, 1))),
            "norm1_w": bf((1.0 + 0.1 * n(HD)) * s),
            "qkv_w": bf(n((3 * HD, HD)) / np.sqrt(HD) / s[None, :]),
            "qkv_b": bf(0.1 * n(3 * HD)),
            "qn_w": bf(1.0 + 0.1 * n(HEAD)), "qn_b": bf(0.1 * n(HEAD)),
            "kn_w": bf(1.0 + 0.1 * n(HEAD)), "kn_b": bf(0.1 * n(HEAD))}


def reference(x, norm1_w, qkv_w, qkv_b, qn_w, qn_b, kn_w, kn_b):
    h1 = rms_in(f64(x), f64(norm1_w)).reshape(B, HD, P)
    qkv = (mxq(f64(qkv_w), 1, "e4m3") @ mxq(h1, 1, "e4m3")) + f64(qkv_b)[None, :, None]
    t = qkv.reshape(B, NH, 3 * HEAD, H, W).transpose(0, 1, 3, 4, 2)
    q, k, v = np.split(t, 3, axis=-1)
    q = ln(q, f64(qn_w), f64(qn_b))
    k = ln(k, f64(kn_w), f64(kn_b))
    return q, k, np.ascontiguousarray(v)

@@ -1,0 +1,391 @@
+from contextlib import ExitStack
+
+import concourse.masks as masks
+import concourse.mybir as mybir
+
+F32 = mybir.dt.float32
+BF16 = mybir.dt.bfloat16
+U32 = mybir.dt.uint32
+U8 = mybir.dt.uint8
+I32 = mybir.dt.int32
+FP8X4 = mybir.dt.float8_e4m3fn_x4
+ALU = mybir.AluOpType
+ACT = mybir.ActivationFunctionType
+
+P = 128
+FLOPS = 2 * 3072 * 1024 * 1024
+MANUAL = True
+
+Q0, K0, Q1, K1, V0, V1 = (0, 0), (1, 0), (0, 1), (1, 1), (2, 0), (2, 1)
+LOAD_ORDER = (Q0, K0, Q1, K1, V0, V1)
+QK_UNITS = ((Q0, 0), (K0, 0), (Q1, 0), (K1, 0), (Q0, 1), (K0, 1), (Q1, 1), (K1, 1))
+
+
+def tile_axialattentionblock_pa_kernel(
+    tc, x, norm1_w, qkv_w, qkv_b, qn_w, qn_b, kn_w, kn_b, out_0, out_1, out_2
+):
+    nc = tc.nc
+    outs = (out_0, out_1, out_2)
+    with ExitStack() as ctx:
+        const = ctx.enter_context(tc.tile_pool(name="const", bufs=1))
+        wgp = ctx.enter_context(tc.tile_pool(name="wgp", bufs=3))
+        hgp = ctx.enter_context(tc.tile_pool(name="hgp", bufs=2))
+        small = ctx.enter_context(tc.tile_pool(name="small", bufs=4))
+        zp = ctx.enter_context(tc.tile_pool(name="zp", bufs=12))
+        op = ctx.enter_context(tc.tile_pool(name="op", bufs=3))
+        vp = ctx.enter_context(tc.tile_pool(name="vp", bufs=2))
+        jp = ctx.enter_context(tc.tile_pool(name="jp", bufs=2))
+        psc = ctx.enter_context(tc.psum_pool(name="psc", bufs=1))
+        psx = ctx.enter_context(tc.psum_pool(name="psx", bufs=4))
+        psa = ctx.enter_context(tc.psum_pool(name="psa", bufs=3))
+        if MANUAL:
+            ctx.enter_context(tc.manual_schedule())
+
+        x_sb = const.tile([P, 2, 4, 1024], BF16, name="x_sb")
+        b_bc = const.tile([P, 8, 3, P], BF16, name="b_bc")
+        w_view = qkv_w.rearrange("(n t p) k -> t p n k", t=3, p=P)
+        wraw = {}
+
+        def load_x(b, g):
+            nc.sync.dma_start(
+                out=x_sb[:, b, 2 * g : 2 * g + 2, :],
+                in_=x[b].rearrange("(r q e) h w -> q r (e h w)", r=4, e=2)[:, 2 * g : 2 * g + 2, :],
+            )
+
+        def load_w(chunk):
+            kind, half = chunk
+            wr = const.tile([P, 4, 1024], BF16, name="wraw%d%d" % chunk)
+            nc.sync.dma_start(out=wr[:], in_=w_view[kind, :, 4 * half : 4 * half + 4, :])
+            wraw[chunk] = wr
+
+        load_x(0, 0)
+        load_x(0, 1)
+        load_w(Q0)
+        load_w(K0)
+        nc.sync.dma_start(
+            out=b_bc[:].rearrange("q n t c -> q (n t c)"), in_=qkv_b.partition_broadcast(P)
+        )
+        load_w(Q1)
+        load_w(K1)
+        load_x(1, 0)
+        load_x(1, 1)
+        load_w(V0)
+        load_w(V1)
+
+        wrow = const.tile([P, 512], BF16, name="wrow")
+        nc.vector.memset(wrow[:].bitcast(I32), 0)
+        for k, vec in enumerate((qn_w, kn_w, qn_b, kn_b)):
+            nc.scalar.dma_start(
+                out=wrow[0:1, P * k : P * (k + 1)], in_=vec.rearrange("(o n) -> o n", o=1)
+            )
+        nw = const.tile([P, 8], BF16, name="nw")
+        with nc.allow_non_contiguous_dma(reason="1024 gains, a pair to a piece"):
+            nc.scalar.dma_start(
+                out=nw[:].rearrange("q (r e) -> q r e", e=2),
+                in_=norm1_w.rearrange("(r q e) -> q r e", r=4, e=2),
+            )
+
+        ones = const.tile([P, P], BF16, name="ones")
+        nc.vector.memset(ones[:], 1.0)
+        one1 = const.tile([P, 1], F32, name="one1")
+        nc.vector.memset(one1[:], 1.0)
+        eps = const.tile([P, 1], F32, name="eps")
+        nc.vector.memset(eps[:], 1e-5)
+        warm = const.tile([P, 1], F32, name="warm")
+        nc.scalar.activation(out=warm[:], in_=one1[:], func=ACT.Sqrt)
+        ident = const.tile([P, P], F32, name="ident")
+        masks.make_identity(nc, ident[:])
+
+        lnc = psc.tile([P, 512], F32, name="lnc")
+        nc.tensor.matmul(out=lnc[:], lhsT=ones[:], rhs=wrow[:], start=True, stop=True)
+
+        st = const.tile([P, 2, 8, 6], F32, name="st")
+        xsc = {}
+        hgs = {}
+        hc = {}
+        hs = {}
+
+        def x_stats(b):
+            for s in range(8):
+                r, e = divmod(s, 2)
+                nc.vector.bn_stats(out=st[:, b, s, :], in_=x_sb[:, b, r, 512 * e : 512 * (e + 1)])
+
+        def x_small(b):
+            d = small.tile([P, 8], F32, name="xd")
+            nc.vector.tensor_tensor(out=d[:], in0=st[:, b, :, 1], in1=st[:, b, :, 4], op=ALU.subtract)
+            d2 = small.tile([P, 8], F32, name="xd2")
+            nc.vector.tensor_tensor(out=d2[:], in0=d[:], in1=d[:], op=ALU.mult)
+            m2 = small.tile([P, 8], F32, name="xm2")
+            nc.vector.tensor_tensor(out=m2[:], in0=st[:, b, :, 2], in1=st[:, b, :, 5], op=ALU.add)
+            ss = small.tile([P, 8], F32, name="xss")
+            nc.vector.scalar_tensor_tensor(
+                out=ss[:], in0=d2[:], scalar=128.0, in1=m2[:], op0=ALU.mult, op1=ALU.add
+            )
+            sd = small.tile([P, 8], F32, name="xsd")
+            nc.scalar.activation(out=sd[:], in_=ss[:], func=ACT.Sqrt, scale=1.0 / 511.0)
+            den = small.tile([P, 8], F32, name="xden")
+            nc.vector.tensor_scalar_add(out=den[:], in0=sd[:], scalar1=1e-8)
+            rec = small.tile([P, 8], F32, name="xrec")
+            nc.vector.reciprocal(out=rec[:], in_=den[:])
+            sc = small.tile([P, 8], F32, name="xsc")
+            nc.vector.tensor_tensor(out=sc[:], in0=rec[:], in1=nw[:], op=ALU.mult)
+            xsc[b] = sc
+
+        def x_scale(b, g):
+            hg = hgp.tile([P, 2048], BF16, name="hg", align_bytes=64)
+            nc.vector.tensor_tensor(
+                out=hg[:].rearrange("q (i p t) -> q i p t", i=4, t=4),
+                in0=x_sb[:, b, 2 * g : 2 * g + 2, :].rearrange("q u (e p i) -> q i p (u e)", e=2, i=4),
+                in1=xsc[b][:, 4 * g : 4 * g + 4].unsqueeze(1).unsqueeze(1).to_broadcast([P, 4, P, 4]),
+                op=ALU.mult,
+            )
+            hgs[(b, g)] = hg
+
+        def x_quant(b, g):
+            codes = const.tile([P, 512], U32, name="hc%d%d" % (b, g), align_bytes=64)
+            scales = const.tile([P, 512], U8, name="hs%d%d" % (b, g), align_bytes=64)
+            nc.vector.quantize_mx(out=codes[:].bitcast(FP8X4), scales=scales[:], in_=hgs[(b, g)][:])
+            hc[(b, g)] = codes
+            hs[(b, g)] = scales
+
+        wgs = {}
+        wc = {}
+        ws = {}
+
+        def w_turn(chunk):
+            wrf = wraw[chunk][:].bitcast(F32)
+            wg = wgp.tile([P, 2, 2048], BF16, name="wg", align_bytes=64)
+            wgf = wg[:].bitcast(F32)
+            for g in range(2):
+                for h in range(2):
+                    tp = psx.tile([P, 2, 2, P], F32, tag="aux", name="tp")
+                    for u in range(2):
+                        for nn in range(2):
+                            c0 = P * (2 * g + u)
+                            nc.tensor.transpose(
+                                out=tp[:, u, nn, :],
+                                in_=wrf[:, 2 * h + nn, c0 : c0 + P],
+                                identity=ident[:],
+                            )
+                    nc.scalar.copy(
+                        out=wgf[:, g, 512 * h : 512 * (h + 1)].rearrange("q (o u) -> q o u", u=2),
+                        in_=tp[:].rearrange("q u n p -> q (n p) u"),
+                    )
+            wgs[chunk] = wg
+            wc[chunk] = const.tile([P, 2, 512], U32, name="wc%d%d" % chunk, align_bytes=64)
+            ws[chunk] = const.tile([P, 2, 512], U8, name="ws%d%d" % chunk, align_bytes=64)
+
+        def w_quant(chunk, g):
+            nc.vector.quantize_mx(
+                out=wc[chunk][:, g, :].bitcast(FP8X4),
+                scales=ws[chunk][:, g, :],
+                in_=wgs[chunk][:, g, :],
+            )
+
+        def product(acc, chunk, b, i):
+            for g in range(2):
+                nc.tensor.matmul_mx(
+                    out=acc[:],
+                    lhsT=hc[(b, g)][:, P * i : P * (i + 1)].bitcast(FP8X4),
+                    lhsT_scale=hs[(b, g)][:, P * i : P * (i + 1)],
+                    rhs=wc[chunk][:, g, :].bitcast(FP8X4),
+                    rhs_scale=ws[chunk][:, g, :],
+                    start=(g == 0),
+                    stop=(g == 1),
+                )
+
+        def bias_of(chunk):
+            kind, half = chunk
+            return b_bc[:, 4 * half : 4 * half + 4, kind, :]
+
+        def store(chunk, b, tile_):
+            kind, half = chunk
+            nc.sync.dma_start(
+                out=outs[kind][b, 4 * half : 4 * half + 4].rearrange("n h (w i) c -> (h w) n (i c)", i=4),
+                in_=tile_[:].rearrange("q n i c -> q n (i c)"),
+            )
+
+        def v_unit(chunk, b):
+            vst = vp.tile([P, 4, 4, P], F32, name="vst")
+            for i in range(4):
+                acc = psx.tile([P, 512], F32, tag="aux", name="vacc")
+                product(acc, chunk, b, i)
+                nc.vector.tensor_tensor(
+                    out=vst[:, :, i, :],
+                    in0=acc[:].rearrange("q (n c) -> q n c", c=P),
+                    in1=bias_of(chunk),
+                    op=ALU.add,
+                )
+            store(chunk, b, vst)
+
+        sumb = const.tile([P, 16], F32, name="sumb")
+        nsb = const.tile([P, 16], F32, name="nsb")
+
+        def bias_sums():
+            for kind in range(2):
+                for n in range(8):
+                    junk = jp.tile([P, P], F32, name="junk")
+                    nc.scalar.activation(
+                        out=junk[:],
+                        in_=b_bc[:, n, kind, :],
+                        func=ACT.Identity,
+                        accum_out=sumb[:, 8 * kind + n : 8 * kind + n + 1],
+                    )
+            nc.vector.tensor_scalar_mul(out=nsb[:], in0=sumb[:], scalar1=-1.0 / 128.0)
+
+        S = {}
+
+        def stage_e(p):
+            chunk, b = QK_UNITS[p]
+            su = small.tile([P, 16], F32, name="su")
+            zs = []
+            for i in range(4):
+                acc = psa.tile([P, 512], F32, name="acc")
+                product(acc, chunk, b, i)
+                z = zp.tile([P, 512], F32, name="z")
+                for n in range(4):
+                    nc.scalar.activation(
+                        out=z[:, P * n : P * (n + 1)],
+                        in_=acc[:, P * n : P * (n + 1)],
+                        func=ACT.Identity,
+                        accum_out=su[:, 4 * i + n : 4 * i + n + 1],
+                    )
+                nc.gpsimd.tensor_tensor(
+                    out=z[:].rearrange("q (n c) -> q n c", c=P),
+                    in0=z[:].rearrange("q (n c) -> q n c", c=P),
+                    in1=bias_of(chunk),
+                    op=ALU.add,
+                )
+                zs.append(z)
+            S[p] = {"su": su, "zs": zs}
+
+        def stage_n(p):
+            (kind, half), b = QK_UNITS[p]
+            negm = small.tile([P, 16], F32, name="negm")
+            c0 = 8 * kind + 4 * half
+            nc.vector.scalar_tensor_tensor(
+                out=negm[:].rearrange("q (i n) -> q i n", n=4),
+                in0=S[p]["su"][:].rearrange("q (i n) -> q i n", n=4),
+                scalar=-1.0 / 128.0,
+                in1=nsb[:, c0 : c0 + 4].unsqueeze(1).to_broadcast([P, 4, 4]),
+                op0=ALU.mult,
+                op1=ALU.add,
+            )
+            S[p]["negm"] = negm
+
+        def stage_ms(p):
+            negm = S[p]["negm"]
+            ssq = small.tile([P, 16], F32, name="ssq")
+            for i in range(4):
+                for n in range(4):
+                    k = 4 * i + n
+                    junk = jp.tile([P, P], F32, name="junk")
+                    nc.scalar.activation(
+                        out=junk[:],
+                        in_=S[p]["zs"][i][:, P * n : P * (n + 1)],
+                        func=ACT.Square,
+                        bias=negm[:, k : k + 1],
+                        accum_out=ssq[:, k : k + 1],
+                    )
+            sd = small.tile([P, 16], F32, name="sd")
+            nc.scalar.activation(out=sd[:], in_=ssq[:], func=ACT.Sqrt, bias=eps[:], scale=1.0 / 128.0)
+            S[p]["sd"] = sd
+
+        def stage_mv(p):
+            (kind, half), b = QK_UNITS[p]
+            negm = S[p]["negm"]
+            ost = op.tile([P, 4, 4, P], F32, name="ost")
+            for i in range(4):
+                for n in range(4):
+                    k = 4 * i + n
+                    nc.vector.scalar_tensor_tensor(
+                        out=ost[:, n, i, :],
+                        in0=S[p]["zs"][i][:, P * n : P * (n + 1)],
+                        scalar=negm[:, k : k + 1],
+                        in1=lnc[:, P * kind : P * (kind + 1)],
+                        op0=ALU.add,
+                        op1=ALU.mult,
+                    )
+            S[p]["ost"] = ost
+
+        def stage_f(p, by_head):
+            chunk, b = QK_UNITS[p]
+            kind, half = chunk
+            ost = S[p]["ost"]
+            rs = small.tile([P, 16], F32, name="rs")
+            nc.vector.reciprocal(out=rs[:], in_=S[p]["sd"][:])
+            for n in range(4):
+                for i in range(4):
+                    k = 4 * i + n
+                    nc.vector.scalar_tensor_tensor(
+                        out=ost[:, n, i, :],
+                        in0=ost[:, n, i, :],
+                        scalar=rs[:, k : k + 1],
+                        in1=lnc[:, 256 + P * kind : 256 + P * (kind + 1)],
+                        op0=ALU.mult,
+                        op1=ALU.add,
+                    )
+                if by_head:
+                    nc.sync.dma_start(
+                        out=outs[kind][b, 4 * half + n].rearrange("h (w i) c -> (h w) (i c)", i=4),
+                        in_=ost[:, n].rearrange("q i c -> q (i c)"),
+                    )
+            if not by_head:
+                store(chunk, b, ost)
+
+        x_stats(0)
+        x_small(0)
+        w_turn(Q0)
+        x_scale(0, 0)
+        w_quant(Q0, 0)
+        x_quant(0, 0)
+        x_scale(0, 1)
+        w_quant(Q0, 1)
+        x_quant(0, 1)
+        w_turn(K0)
+        bias_sums()
+        w_quant(K0, 0)
+        w_quant(K0, 1)
+        w_turn(Q1)
+
+        def filler(p):
+            if p == 0:
+                w_turn(K1)
+                w_quant(Q1, 0)
+                w_quant(Q1, 1)
+                x_stats(1)
+                x_small(1)
+            elif p == 1:
+                w_turn(V0)
+                x_scale(1, 0)
+                w_quant(K1, 0)
+                w_quant(K1, 1)
+                x_quant(1, 0)
+            elif p == 2:
+                w_turn(V1)
+                x_scale(1, 1)
+                w_quant(V0, 0)
+                w_quant(V0, 1)
+                x_quant(1, 1)
+            elif p == 3:
+                w_quant(V1, 0)
+                w_quant(V1, 1)
+                v_unit(V0, 0)
+            elif p == 4:
+                v_unit(V1, 0)
+            elif p == 5:
+                v_unit(V0, 1)
+            elif p == 6:
+                v_unit(V1, 1)
+
+        for p in range(10):
+            if p < 8:
+                stage_e(p)
+            if 0 <= p - 2 < 8:
+                stage_f(p - 2, p - 2 == 7)
+            if 0 <= p - 1 < 8:
+                stage_mv(p - 1)
+                stage_ms(p - 1)
+            if p < 8:
+                stage_n(p)
+            filler(p)

@@ -36,13 +36,13 @@ def tile_axialattentionblock_pa_kernel(
         vp = ctx.enter_context(tc.tile_pool(name="vp", bufs=2))
         jp = ctx.enter_context(tc.tile_pool(name="jp", bufs=2))
         psc = ctx.enter_context(tc.psum_pool(name="psc", bufs=1))
-        psx = ctx.enter_context(tc.psum_pool(name="psx", bufs=4))
-        psa = ctx.enter_context(tc.psum_pool(name="psa", bufs=3))
+        psx = ctx.enter_context(tc.psum_pool(name="psx", bufs=3))
+        psa = ctx.enter_context(tc.psum_pool(name="psa", bufs=4))
         if MANUAL:
             ctx.enter_context(tc.manual_schedule())
 
         x_sb = const.tile([P, 2, 4, 1024], BF16, name="x_sb")
-        b_bc = const.tile([P, 8, 3, P], BF16, name="b_bc")
+        b_bc = const.tile([P, 3, 8, P], F32, name="b_bc")
         w_view = qkv_w.rearrange("(n t p) k -> t p n k", t=3, p=P)
         wraw = {}
 
@@ -61,17 +61,17 @@ def tile_axialattentionblock_pa_kernel(
         load_x(0, 0)
         load_x(0, 1)
         load_w(Q0)
-        load_w(K0)
-        nc.sync.dma_start(
-            out=b_bc[:].rearrange("q n t c -> q (n t c)"), in_=qkv_b.partition_broadcast(P)
-        )
-        load_w(Q1)
-        load_w(K1)
         load_x(1, 0)
         load_x(1, 1)
+        load_w(K0)
+        load_w(Q1)
+        load_w(K1)
         load_w(V0)
         load_w(V1)
 
+        brow = const.tile([P, 3072], BF16, name="brow")
+        nc.vector.memset(brow[:].bitcast(I32), 0)
+        nc.scalar.dma_start(out=brow[0:1, :], in_=qkv_b.rearrange("(o n) -> o n", o=1))
         wrow = const.tile([P, 512], BF16, name="wrow")
         nc.vector.memset(wrow[:].bitcast(I32), 0)
         for k, vec in enumerate((qn_w, kn_w, qn_b, kn_b)):
@@ -99,8 +99,27 @@ def tile_axialattentionblock_pa_kernel(
         lnc = psc.tile([P, 512], F32, name="lnc")
         nc.tensor.matmul(out=lnc[:], lhsT=ones[:], rhs=wrow[:], start=True, stop=True)
 
+        sumb = const.tile([P, 24], F32, name="sumb")
+        nsb = const.tile([P, 24], F32, name="nsb")
+        for j in range(6):
+            bps = psa.tile([P, 512], F32, tag="acc", name="bps")
+            nc.tensor.matmul(
+                out=bps[:], lhsT=ones[:], rhs=brow[:, 512 * j : 512 * (j + 1)], start=True, stop=True
+            )
+            for gl in range(4):
+                head, kind = divmod(4 * j + gl, 3)
+                col = 8 * kind + head
+                nc.scalar.activation(
+                    out=b_bc[:, kind, head, :],
+                    in_=bps[:, P * gl : P * (gl + 1)],
+                    func=ACT.Identity,
+                    accum_out=sumb[:, col : col + 1],
+                )
+
         st = const.tile([P, 2, 8, 6], F32, name="st")
         xsc = {}
+        xss = {}
+        xsd = {}
         hgs = {}
         hc = {}
         hs = {}
@@ -121,8 +140,15 @@ def tile_axialattentionblock_pa_kernel(
             nc.vector.scalar_tensor_tensor(
                 out=ss[:], in0=d2[:], scalar=128.0, in1=m2[:], op0=ALU.mult, op1=ALU.add
             )
+            xss[b] = ss
+
+        def x_small_b(b):
             sd = small.tile([P, 8], F32, name="xsd")
-            nc.scalar.activation(out=sd[:], in_=ss[:], func=ACT.Sqrt, scale=1.0 / 511.0)
+            nc.scalar.activation(out=sd[:], in_=xss[b][:], func=ACT.Sqrt, scale=1.0 / 511.0)
+            xsd[b] = sd
+
+        def x_small_c(b):
+            sd = xsd[b]
             den = small.tile([P, 8], F32, name="xden")
             nc.vector.tensor_scalar_add(out=den[:], in0=sd[:], scalar1=1e-8)
             rec = small.tile([P, 8], F32, name="xrec")
@@ -196,7 +222,7 @@ def tile_axialattentionblock_pa_kernel(
 
         def bias_of(chunk):
             kind, half = chunk
-            return b_bc[:, 4 * half : 4 * half + 4, kind, :]
+            return b_bc[:, kind, 4 * half : 4 * half + 4, :]
 
         def store(chunk, b, tile_):
             kind, half = chunk
@@ -218,30 +244,23 @@ def tile_axialattentionblock_pa_kernel(
                 )
             store(chunk, b, vst)
 
-        sumb = const.tile([P, 16], F32, name="sumb")
-        nsb = const.tile([P, 16], F32, name="nsb")
-
-        def bias_sums():
-            for kind in range(2):
-                for n in range(8):
-                    junk = jp.tile([P, P], F32, name="junk")
-                    nc.scalar.activation(
-                        out=junk[:],
-                        in_=b_bc[:, n, kind, :],
-                        func=ACT.Identity,
-                        accum_out=sumb[:, 8 * kind + n : 8 * kind + n + 1],
-                    )
-            nc.vector.tensor_scalar_mul(out=nsb[:], in0=sumb[:], scalar1=-1.0 / 128.0)
-
         S = {}
 
-        def stage_e(p):
+        def stage_pe(p):
+            chunk, b = QK_UNITS[p]
+            accs = []
+            for i in range(4):
+                acc = psa.tile([P, 512], F32, tag="acc", name="acc")
+                product(acc, chunk, b, i)
+                accs.append(acc)
+            S[p] = {"accs": accs}
+
+        def stage_sg(p):
             chunk, b = QK_UNITS[p]
             su = small.tile([P, 16], F32, name="su")
             zs = []
             for i in range(4):
-                acc = psa.tile([P, 512], F32, name="acc")
-                product(acc, chunk, b, i)
+                acc = S[p]["accs"][i]
                 z = zp.tile([P, 512], F32, name="z")
                 for n in range(4):
                     nc.scalar.activation(
@@ -257,7 +276,8 @@ def tile_axialattentionblock_pa_kernel(
                     op=ALU.add,
                 )
                 zs.append(z)
-            S[p] = {"su": su, "zs": zs}
+            S[p]["su"] = su
+            S[p]["zs"] = zs
 
         def stage_n(p):
             (kind, half), b = QK_UNITS[p]
@@ -335,6 +355,9 @@ def tile_axialattentionblock_pa_kernel(
 
         x_stats(0)
         x_small(0)
+        x_small_b(0)
+        x_small_c(0)
+        nc.vector.tensor_scalar_mul(out=nsb[:], in0=sumb[:], scalar1=-1.0 / 128.0)
         w_turn(Q0)
         x_scale(0, 0)
         w_quant(Q0, 0)
@@ -343,18 +366,19 @@ def tile_axialattentionblock_pa_kernel(
         w_quant(Q0, 1)
         x_quant(0, 1)
         w_turn(K0)
-        bias_sums()
         w_quant(K0, 0)
         w_quant(K0, 1)
-        w_turn(Q1)
+        x_stats(1)
+        x_small(1)
+        stage_pe(0)
 
         def filler(p):
             if p == 0:
+                w_turn(Q1)
                 w_turn(K1)
                 w_quant(Q1, 0)
                 w_quant(Q1, 1)
-                x_stats(1)
-                x_small(1)
+                x_small_b(1)
             elif p == 1:
                 w_turn(V0)
                 x_scale(1, 0)
@@ -380,11 +404,15 @@ def tile_axialattentionblock_pa_kernel(
 
         for p in range(10):
             if p < 8:
-                stage_e(p)
+                stage_sg(p)
+            if p + 1 < 8:
+                stage_pe(p + 1)
             if 0 <= p - 2 < 8:
                 stage_f(p - 2, p - 2 == 7)
             if 0 <= p - 1 < 8:
                 stage_mv(p - 1)
+                if p == 1:
+                    x_small_c(1)
                 stage_ms(p - 1)
             if p < 8:
                 stage_n(p)

@@ -14,7 +14,7 @@ ACT = mybir.ActivationFunctionType
 
 P = 128
 FLOPS = 2 * 3072 * 1024 * 1024
-MANUAL = True
+MANUAL = False
 
 Q0, K0, Q1, K1, V0, V1 = (0, 0), (1, 0), (0, 1), (1, 1), (2, 0), (2, 1)
 LOAD_ORDER = (Q0, K0, Q1, K1, V0, V1)
@@ -30,19 +30,20 @@ def tile_axialattentionblock_pa_kernel(
         const = ctx.enter_context(tc.tile_pool(name="const", bufs=1))
         wgp = ctx.enter_context(tc.tile_pool(name="wgp", bufs=3))
         hgp = ctx.enter_context(tc.tile_pool(name="hgp", bufs=2))
+        xsp = ctx.enter_context(tc.tile_pool(name="xsp", bufs=2))
         small = ctx.enter_context(tc.tile_pool(name="small", bufs=4))
         zp = ctx.enter_context(tc.tile_pool(name="zp", bufs=12))
         op = ctx.enter_context(tc.tile_pool(name="op", bufs=3))
         vp = ctx.enter_context(tc.tile_pool(name="vp", bufs=2))
         jp = ctx.enter_context(tc.tile_pool(name="jp", bufs=2))
         psc = ctx.enter_context(tc.psum_pool(name="psc", bufs=1))
-        psx = ctx.enter_context(tc.psum_pool(name="psx", bufs=3))
-        psa = ctx.enter_context(tc.psum_pool(name="psa", bufs=4))
+        psx = ctx.enter_context(tc.psum_pool(name="psx", bufs=4))
+        psa = ctx.enter_context(tc.psum_pool(name="psa", bufs=3))
         if MANUAL:
             ctx.enter_context(tc.manual_schedule())
 
         x_sb = const.tile([P, 2, 4, 1024], BF16, name="x_sb")
-        b_bc = const.tile([P, 3, 8, P], F32, name="b_bc")
+        b_bc = const.tile([P, 8, 3, P], BF16, name="b_bc")
         w_view = qkv_w.rearrange("(n t p) k -> t p n k", t=3, p=P)
         wraw = {}
 
@@ -61,17 +62,17 @@ def tile_axialattentionblock_pa_kernel(
         load_x(0, 0)
         load_x(0, 1)
         load_w(Q0)
-        load_x(1, 0)
-        load_x(1, 1)
         load_w(K0)
+        nc.sync.dma_start(
+            out=b_bc[:].rearrange("q n t c -> q (n t c)"), in_=qkv_b.partition_broadcast(P)
+        )
         load_w(Q1)
         load_w(K1)
+        load_x(1, 0)
+        load_x(1, 1)
         load_w(V0)
         load_w(V1)
 
-        brow = const.tile([P, 3072], BF16, name="brow")
-        nc.vector.memset(brow[:].bitcast(I32), 0)
-        nc.scalar.dma_start(out=brow[0:1, :], in_=qkv_b.rearrange("(o n) -> o n", o=1))
         wrow = const.tile([P, 512], BF16, name="wrow")
         nc.vector.memset(wrow[:].bitcast(I32), 0)
         for k, vec in enumerate((qn_w, kn_w, qn_b, kn_b)):
@@ -99,27 +100,8 @@ def tile_axialattentionblock_pa_kernel(
         lnc = psc.tile([P, 512], F32, name="lnc")
         nc.tensor.matmul(out=lnc[:], lhsT=ones[:], rhs=wrow[:], start=True, stop=True)
 
-        sumb = const.tile([P, 24], F32, name="sumb")
-        nsb = const.tile([P, 24], F32, name="nsb")
-        for j in range(6):
-            bps = psa.tile([P, 512], F32, tag="acc", name="bps")
-            nc.tensor.matmul(
-                out=bps[:], lhsT=ones[:], rhs=brow[:, 512 * j : 512 * (j + 1)], start=True, stop=True
-            )
-            for gl in range(4):
-                head, kind = divmod(4 * j + gl, 3)
-                col = 8 * kind + head
-                nc.scalar.activation(
-                    out=b_bc[:, kind, head, :],
-                    in_=bps[:, P * gl : P * (gl + 1)],
-                    func=ACT.Identity,
-                    accum_out=sumb[:, col : col + 1],
-                )
-
         st = const.tile([P, 2, 8, 6], F32, name="st")
         xsc = {}
-        xss = {}
-        xsd = {}
         hgs = {}
         hc = {}
         hs = {}
@@ -140,15 +122,8 @@ def tile_axialattentionblock_pa_kernel(
             nc.vector.scalar_tensor_tensor(
                 out=ss[:], in0=d2[:], scalar=128.0, in1=m2[:], op0=ALU.mult, op1=ALU.add
             )
-            xss[b] = ss
-
-        def x_small_b(b):
             sd = small.tile([P, 8], F32, name="xsd")
-            nc.scalar.activation(out=sd[:], in_=xss[b][:], func=ACT.Sqrt, scale=1.0 / 511.0)
-            xsd[b] = sd
-
-        def x_small_c(b):
-            sd = xsd[b]
+            nc.scalar.activation(out=sd[:], in_=ss[:], func=ACT.Sqrt, scale=1.0 / 511.0)
             den = small.tile([P, 8], F32, name="xden")
             nc.vector.tensor_scalar_add(out=den[:], in0=sd[:], scalar1=1e-8)
             rec = small.tile([P, 8], F32, name="xrec")
@@ -159,6 +134,23 @@ def tile_axialattentionblock_pa_kernel(
 
         def x_scale(b, g):
             hg = hgp.tile([P, 2048], BF16, name="hg", align_bytes=64)
+            hgs[(b, g)] = hg
+            if (b, g) != (0, 0):
+                xs = xsp.tile([P, 4, 512], BF16, name="xs")
+                for t in range(4):
+                    nc.gpsimd.tensor_scalar(
+                        out=xs[:, t, :],
+                        in0=x_sb[:, b, 2 * g + t // 2, 512 * (t % 2) : 512 * (t % 2 + 1)],
+                        scalar1=xsc[b][:, 4 * g + t : 4 * g + t + 1],
+                        scalar2=0.0,
+                        op0=ALU.mult,
+                        op1=ALU.add,
+                    )
+                nc.vector.tensor_copy(
+                    out=hg[:].rearrange("q (i p t) -> q i p t", i=4, t=4),
+                    in_=xs[:].rearrange("q t (p i) -> q i p t", i=4),
+                )
+                return
             nc.vector.tensor_tensor(
                 out=hg[:].rearrange("q (i p t) -> q i p t", i=4, t=4),
                 in0=x_sb[:, b, 2 * g : 2 * g + 2, :].rearrange("q u (e p i) -> q i p (u e)", e=2, i=4),
@@ -222,7 +214,7 @@ def tile_axialattentionblock_pa_kernel(
 
         def bias_of(chunk):
             kind, half = chunk
-            return b_bc[:, kind, 4 * half : 4 * half + 4, :]
+            return b_bc[:, 4 * half : 4 * half + 4, kind, :]
 
         def store(chunk, b, tile_):
             kind, half = chunk
@@ -244,23 +236,30 @@ def tile_axialattentionblock_pa_kernel(
                 )
             store(chunk, b, vst)
 
+        sumb = const.tile([P, 16], F32, name="sumb")
+        nsb = const.tile([P, 16], F32, name="nsb")
+
+        def bias_sums():
+            for kind in range(2):
+                for n in range(8):
+                    junk = jp.tile([P, P], F32, name="junk")
+                    nc.scalar.activation(
+                        out=junk[:],
+                        in_=b_bc[:, n, kind, :],
+                        func=ACT.Identity,
+                        accum_out=sumb[:, 8 * kind + n : 8 * kind + n + 1],
+                    )
+            nc.vector.tensor_scalar_mul(out=nsb[:], in0=sumb[:], scalar1=-1.0 / 128.0)
+
         S = {}
 
-        def stage_pe(p):
-            chunk, b = QK_UNITS[p]
-            accs = []
-            for i in range(4):
-                acc = psa.tile([P, 512], F32, tag="acc", name="acc")
-                product(acc, chunk, b, i)
-                accs.append(acc)
-            S[p] = {"accs": accs}
-
-        def stage_sg(p):
+        def stage_e(p):
             chunk, b = QK_UNITS[p]
             su = small.tile([P, 16], F32, name="su")
             zs = []
             for i in range(4):
-                acc = S[p]["accs"][i]
+                acc = psa.tile([P, 512], F32, name="acc")
+                product(acc, chunk, b, i)
                 z = zp.tile([P, 512], F32, name="z")
                 for n in range(4):
                     nc.scalar.activation(
@@ -276,8 +275,7 @@ def tile_axialattentionblock_pa_kernel(
                     op=ALU.add,
                 )
                 zs.append(z)
-            S[p]["su"] = su
-            S[p]["zs"] = zs
+            S[p] = {"su": su, "zs": zs}
 
         def stage_n(p):
             (kind, half), b = QK_UNITS[p]
@@ -355,9 +353,6 @@ def tile_axialattentionblock_pa_kernel(
 
         x_stats(0)
         x_small(0)
-        x_small_b(0)
-        x_small_c(0)
-        nc.vector.tensor_scalar_mul(out=nsb[:], in0=sumb[:], scalar1=-1.0 / 128.0)
         w_turn(Q0)
         x_scale(0, 0)
         w_quant(Q0, 0)
@@ -366,19 +361,18 @@ def tile_axialattentionblock_pa_kernel(
         w_quant(Q0, 1)
         x_quant(0, 1)
         w_turn(K0)
+        bias_sums()
         w_quant(K0, 0)
         w_quant(K0, 1)
-        x_stats(1)
-        x_small(1)
-        stage_pe(0)
+        w_turn(Q1)
 
         def filler(p):
             if p == 0:
-                w_turn(Q1)
                 w_turn(K1)
                 w_quant(Q1, 0)
                 w_quant(Q1, 1)
-                x_small_b(1)
+                x_stats(1)
+                x_small(1)
             elif p == 1:
                 w_turn(V0)
                 x_scale(1, 0)
@@ -404,15 +398,11 @@ def tile_axialattentionblock_pa_kernel(
 
         for p in range(10):
             if p < 8:
-                stage_sg(p)
-            if p + 1 < 8:
-                stage_pe(p + 1)
+                stage_e(p)
             if 0 <= p - 2 < 8:
                 stage_f(p - 2, p - 2 == 7)
             if 0 <= p - 1 < 8:
                 stage_mv(p - 1)
-                if p == 1:
-                    x_small_c(1)
                 stage_ms(p - 1)
             if p < 8:
                 stage_n(p)

@@ -30,7 +30,6 @@ def tile_axialattentionblock_pa_kernel(
         const = ctx.enter_context(tc.tile_pool(name="const", bufs=1))
         wgp = ctx.enter_context(tc.tile_pool(name="wgp", bufs=3))
         hgp = ctx.enter_context(tc.tile_pool(name="hgp", bufs=2))
-        xsp = ctx.enter_context(tc.tile_pool(name="xsp", bufs=2))
         small = ctx.enter_context(tc.tile_pool(name="small", bufs=4))
         zp = ctx.enter_context(tc.tile_pool(name="zp", bufs=12))
         op = ctx.enter_context(tc.tile_pool(name="op", bufs=3))
@@ -134,23 +133,6 @@ def tile_axialattentionblock_pa_kernel(
 
         def x_scale(b, g):
             hg = hgp.tile([P, 2048], BF16, name="hg", align_bytes=64)
-            hgs[(b, g)] = hg
-            if (b, g) != (0, 0):
-                xs = xsp.tile([P, 4, 512], BF16, name="xs")
-                for t in range(4):
-                    nc.gpsimd.tensor_scalar(
-                        out=xs[:, t, :],
-                        in0=x_sb[:, b, 2 * g + t // 2, 512 * (t % 2) : 512 * (t % 2 + 1)],
-                        scalar1=xsc[b][:, 4 * g + t : 4 * g + t + 1],
-                        scalar2=0.0,
-                        op0=ALU.mult,
-                        op1=ALU.add,
-                    )
-                nc.vector.tensor_copy(
-                    out=hg[:].rearrange("q (i p t) -> q i p t", i=4, t=4),
-                    in_=xs[:].rearrange("q t (p i) -> q i p t", i=4),
-                )
-                return
             nc.vector.tensor_tensor(
                 out=hg[:].rearrange("q (i p t) -> q i p t", i=4, t=4),
                 in0=x_sb[:, b, 2 * g : 2 * g + 2, :].rearrange("q u (e p i) -> q i p (u e)", e=2, i=4),
@@ -236,21 +218,6 @@ def tile_axialattentionblock_pa_kernel(
                 )
             store(chunk, b, vst)
 
-        sumb = const.tile([P, 16], F32, name="sumb")
-        nsb = const.tile([P, 16], F32, name="nsb")
-
-        def bias_sums():
-            for kind in range(2):
-                for n in range(8):
-                    junk = jp.tile([P, P], F32, name="junk")
-                    nc.scalar.activation(
-                        out=junk[:],
-                        in_=b_bc[:, n, kind, :],
-                        func=ACT.Identity,
-                        accum_out=sumb[:, 8 * kind + n : 8 * kind + n + 1],
-                    )
-            nc.vector.tensor_scalar_mul(out=nsb[:], in0=sumb[:], scalar1=-1.0 / 128.0)
-
         S = {}
 
         def stage_e(p):
@@ -261,34 +228,27 @@ def tile_axialattentionblock_pa_kernel(
                 acc = psa.tile([P, 512], F32, name="acc")
                 product(acc, chunk, b, i)
                 z = zp.tile([P, 512], F32, name="z")
-                for n in range(4):
-                    nc.scalar.activation(
-                        out=z[:, P * n : P * (n + 1)],
-                        in_=acc[:, P * n : P * (n + 1)],
-                        func=ACT.Identity,
-                        accum_out=su[:, 4 * i + n : 4 * i + n + 1],
-                    )
-                nc.gpsimd.tensor_tensor(
+                nc.vector.tensor_tensor(
                     out=z[:].rearrange("q (n c) -> q n c", c=P),
-                    in0=z[:].rearrange("q (n c) -> q n c", c=P),
+                    in0=acc[:].rearrange("q (n c) -> q n c", c=P),
                     in1=bias_of(chunk),
                     op=ALU.add,
                 )
+                for n in range(4):
+                    junk = jp.tile([P, P], F32, name="junk")
+                    nc.scalar.activation(
+                        out=junk[:],
+                        in_=z[:, P * n : P * (n + 1)],
+                        func=ACT.Identity,
+                        accum_out=su[:, 4 * i + n : 4 * i + n + 1],
+                    )
                 zs.append(z)
             S[p] = {"su": su, "zs": zs}
 
         def stage_n(p):
             (kind, half), b = QK_UNITS[p]
             negm = small.tile([P, 16], F32, name="negm")
-            c0 = 8 * kind + 4 * half
-            nc.vector.scalar_tensor_tensor(
-                out=negm[:].rearrange("q (i n) -> q i n", n=4),
-                in0=S[p]["su"][:].rearrange("q (i n) -> q i n", n=4),
-                scalar=-1.0 / 128.0,
-                in1=nsb[:, c0 : c0 + 4].unsqueeze(1).to_broadcast([P, 4, 4]),
-                op0=ALU.mult,
-                op1=ALU.add,
-            )
+            nc.vector.tensor_scalar_mul(out=negm[:], in0=S[p]["su"][:], scalar1=-1.0 / 128.0)
             S[p]["negm"] = negm
 
         def stage_ms(p):
@@ -361,7 +321,6 @@ def tile_axialattentionblock_pa_kernel(
         w_quant(Q0, 1)
         x_quant(0, 1)
         w_turn(K0)
-        bias_sums()
         w_quant(K0, 0)
         w_quant(K0, 1)
         w_turn(Q1)

@@ -218,6 +218,21 @@ def tile_axialattentionblock_pa_kernel(
                 )
             store(chunk, b, vst)
 
+        sumb = const.tile([P, 16], F32, name="sumb")
+        nsb = const.tile([P, 16], F32, name="nsb")
+
+        def bias_sums():
+            for kind in range(2):
+                for n in range(8):
+                    junk = jp.tile([P, P], F32, name="junk")
+                    nc.scalar.activation(
+                        out=junk[:],
+                        in_=b_bc[:, n, kind, :],
+                        func=ACT.Identity,
+                        accum_out=sumb[:, 8 * kind + n : 8 * kind + n + 1],
+                    )
+            nc.vector.tensor_scalar_mul(out=nsb[:], in0=sumb[:], scalar1=-1.0 / 128.0)
+
         S = {}
 
         def stage_e(p):
@@ -228,27 +243,34 @@ def tile_axialattentionblock_pa_kernel(
                 acc = psa.tile([P, 512], F32, name="acc")
                 product(acc, chunk, b, i)
                 z = zp.tile([P, 512], F32, name="z")
-                nc.vector.tensor_tensor(
-                    out=z[:].rearrange("q (n c) -> q n c", c=P),
-                    in0=acc[:].rearrange("q (n c) -> q n c", c=P),
-                    in1=bias_of(chunk),
-                    op=ALU.add,
-                )
                 for n in range(4):
-                    junk = jp.tile([P, P], F32, name="junk")
                     nc.scalar.activation(
-                        out=junk[:],
-                        in_=z[:, P * n : P * (n + 1)],
+                        out=z[:, P * n : P * (n + 1)],
+                        in_=acc[:, P * n : P * (n + 1)],
                         func=ACT.Identity,
                         accum_out=su[:, 4 * i + n : 4 * i + n + 1],
                     )
+                nc.gpsimd.tensor_tensor(
+                    out=z[:].rearrange("q (n c) -> q n c", c=P),
+                    in0=z[:].rearrange("q (n c) -> q n c", c=P),
+                    in1=bias_of(chunk),
+                    op=ALU.add,
+                )
                 zs.append(z)
             S[p] = {"su": su, "zs": zs}
 
         def stage_n(p):
             (kind, half), b = QK_UNITS[p]
             negm = small.tile([P, 16], F32, name="negm")
-            nc.vector.tensor_scalar_mul(out=negm[:], in0=S[p]["su"][:], scalar1=-1.0 / 128.0)
+            c0 = 8 * kind + 4 * half
+            nc.vector.scalar_tensor_tensor(
+                out=negm[:].rearrange("q (i n) -> q i n", n=4),
+                in0=S[p]["su"][:].rearrange("q (i n) -> q i n", n=4),
+                scalar=-1.0 / 128.0,
+                in1=nsb[:, c0 : c0 + 4].unsqueeze(1).to_broadcast([P, 4, 4]),
+                op0=ALU.mult,
+                op1=ALU.add,
+            )
             S[p]["negm"] = negm
 
         def stage_ms(p):
@@ -321,6 +343,7 @@ def tile_axialattentionblock_pa_kernel(
         w_quant(Q0, 1)
         x_quant(0, 1)
         w_turn(K0)
+        bias_sums()
         w_quant(K0, 0)
         w_quant(K0, 1)
         w_turn(Q1)

@@ -15,6 +15,7 @@ ACT = mybir.ActivationFunctionType
 P = 128
 FLOPS = 2 * 3072 * 1024 * 1024
 MANUAL = False
+N_UNITS = (0, 1, 2, 3, 4, 5, 6, 7)
 
 Q0, K0, Q1, K1, V0, V1 = (0, 0), (1, 0), (0, 1), (1, 1), (2, 0), (2, 1)
 LOAD_ORDER = (Q0, K0, Q1, K1, V0, V1)
@@ -218,20 +219,30 @@ def tile_axialattentionblock_pa_kernel(
                 )
             store(chunk, b, vst)
 
-        sumb = const.tile([P, 16], F32, name="sumb")
-        nsb = const.tile([P, 16], F32, name="nsb")
+        tree = const.tile([P, 8, 2, 64], F32, name="tree")
+        nsb = const.tile([P, 8, 2], F32, name="nsb")
 
         def bias_sums():
-            for kind in range(2):
-                for n in range(8):
-                    junk = jp.tile([P, P], F32, name="junk")
-                    nc.scalar.activation(
-                        out=junk[:],
-                        in_=b_bc[:, n, kind, :],
-                        func=ACT.Identity,
-                        accum_out=sumb[:, 8 * kind + n : 8 * kind + n + 1],
-                    )
-            nc.vector.tensor_scalar_mul(out=nsb[:], in0=sumb[:], scalar1=-1.0 / 128.0)
+            nc.gpsimd.tensor_tensor(
+                out=tree[:], in0=b_bc[:, :, 0:2, 0:64], in1=b_bc[:, :, 0:2, 64:128], op=ALU.add
+            )
+            width = 32
+            while width >= 1:
+                nc.gpsimd.tensor_tensor(
+                    out=tree[:, :, :, 0:width],
+                    in0=tree[:, :, :, 0:width],
+                    in1=tree[:, :, :, width : 2 * width],
+                    op=ALU.add,
+                )
+                width = width // 2
+            nc.gpsimd.tensor_scalar(
+                out=nsb[:],
+                in0=tree[:, :, :, 0],
+                scalar1=-1.0 / 128.0,
+                scalar2=0.0,
+                op0=ALU.mult,
+                op1=ALU.add,
+            )
 
         S = {}
 
@@ -262,12 +273,11 @@ def tile_axialattentionblock_pa_kernel(
         def stage_n(p):
             (kind, half), b = QK_UNITS[p]
             negm = small.tile([P, 16], F32, name="negm")
-            c0 = 8 * kind + 4 * half
             nc.vector.scalar_tensor_tensor(
                 out=negm[:].rearrange("q (i n) -> q i n", n=4),
                 in0=S[p]["su"][:].rearrange("q (i n) -> q i n", n=4),
                 scalar=-1.0 / 128.0,
-                in1=nsb[:, c0 : c0 + 4].unsqueeze(1).to_broadcast([P, 4, 4]),
+                in1=nsb[:, 4 * half : 4 * half + 4, kind].unsqueeze(1).to_broadcast([P, 4, 4]),
                 op0=ALU.mult,
                 op1=ALU.add,
             )
@@ -292,6 +302,8 @@ def tile_axialattentionblock_pa_kernel(
             S[p]["sd"] = sd
 
         def stage_mv(p):
+            if p in N_UNITS:
+                return
             (kind, half), b = QK_UNITS[p]
             negm = S[p]["negm"]
             ost = op.tile([P, 4, 4, P], F32, name="ost")
@@ -311,9 +323,46 @@ def tile_axialattentionblock_pa_kernel(
         def stage_f(p, by_head):
             chunk, b = QK_UNITS[p]
             kind, half = chunk
-            ost = S[p]["ost"]
             rs = small.tile([P, 16], F32, name="rs")
             nc.vector.reciprocal(out=rs[:], in_=S[p]["sd"][:])
+            if p in N_UNITS:
+                nmr = small.tile([P, 16], F32, name="nmr")
+                nc.vector.tensor_tensor(out=nmr[:], in0=S[p]["negm"][:], in1=rs[:], op=ALU.mult)
+                ost = op.tile([P, 4, 4, P], F32, name="ost")
+                gain = lnc[:, P * kind : P * (kind + 1)].unsqueeze(1)
+                shift = lnc[:, 256 + P * kind : 256 + P * (kind + 1)].unsqueeze(1)
+                for n in range(4):
+                    for i in range(4):
+                        k = 4 * i + n
+                        nc.scalar.activation(
+                            out=ost[:, n, i, :],
+                            in_=S[p]["zs"][i][:, P * n : P * (n + 1)],
+                            func=ACT.Identity,
+                            bias=nmr[:, k : k + 1],
+                            scale=rs[:, k : k + 1],
+                        )
+                    if by_head:
+                        nc.vector.tensor_tensor(
+                            out=ost[:, n], in0=ost[:, n], in1=gain.to_broadcast([P, 4, P]), op=ALU.mult
+                        )
+                        nc.vector.tensor_tensor(
+                            out=ost[:, n], in0=ost[:, n], in1=shift.to_broadcast([P, 4, P]), op=ALU.add
+                        )
+                        nc.sync.dma_start(
+                            out=outs[kind][b, 4 * half + n].rearrange("h (w i) c -> (h w) (i c)", i=4),
+                            in_=ost[:, n].rearrange("q i c -> q (i c)"),
+                        )
+                if not by_head:
+                    flat = ost[:].rearrange("q n i c -> q (n i) c")
+                    nc.vector.tensor_tensor(
+                        out=flat, in0=flat, in1=gain.to_broadcast([P, 16, P]), op=ALU.mult
+                    )
+                    nc.vector.tensor_tensor(
+                        out=flat, in0=flat, in1=shift.to_broadcast([P, 16, P]), op=ALU.add
+                    )
+                    store(chunk, b, ost)
+                return
+            ost = S[p]["ost"]
             for n in range(4):
                 for i in range(4):
                     k = 4 * i + n

@@ -15,7 +15,7 @@ ACT = mybir.ActivationFunctionType
 P = 128
 FLOPS = 2 * 3072 * 1024 * 1024
 MANUAL = False
-N_UNITS = (0, 1, 2, 3, 4, 5, 6, 7)
+N_UNITS = ()
 
 Q0, K0, Q1, K1, V0, V1 = (0, 0), (1, 0), (0, 1), (1, 1), (2, 0), (2, 1)
 LOAD_ORDER = (Q0, K0, Q1, K1, V0, V1)
@@ -31,11 +31,12 @@ def tile_axialattentionblock_pa_kernel(
         const = ctx.enter_context(tc.tile_pool(name="const", bufs=1))
         wgp = ctx.enter_context(tc.tile_pool(name="wgp", bufs=3))
         hgp = ctx.enter_context(tc.tile_pool(name="hgp", bufs=2))
-        small = ctx.enter_context(tc.tile_pool(name="small", bufs=4))
-        zp = ctx.enter_context(tc.tile_pool(name="zp", bufs=12))
+        xsp = ctx.enter_context(tc.tile_pool(name="xsp", bufs=1))
+        small = ctx.enter_context(tc.tile_pool(name="small", bufs=6))
+        zp = ctx.enter_context(tc.tile_pool(name="zp", bufs=16))
         op = ctx.enter_context(tc.tile_pool(name="op", bufs=3))
         vp = ctx.enter_context(tc.tile_pool(name="vp", bufs=2))
-        jp = ctx.enter_context(tc.tile_pool(name="jp", bufs=2))
+        jp = ctx.enter_context(tc.tile_pool(name="jp", bufs=8))
         psc = ctx.enter_context(tc.psum_pool(name="psc", bufs=1))
         psx = ctx.enter_context(tc.psum_pool(name="psx", bufs=4))
         psa = ctx.enter_context(tc.psum_pool(name="psa", bufs=3))
@@ -134,6 +135,21 @@ def tile_axialattentionblock_pa_kernel(
 
         def x_scale(b, g):
             hg = hgp.tile([P, 2048], BF16, name="hg", align_bytes=64)
+            hgs[(b, g)] = hg
+            if (b, g) == (0, 1):
+                xs = xsp.tile([P, 4, 512], BF16, name="xs")
+                for t in range(4):
+                    nc.scalar.activation(
+                        out=xs[:, t, :],
+                        in_=x_sb[:, b, 2 * g + t // 2, 512 * (t % 2) : 512 * (t % 2 + 1)],
+                        func=ACT.Copy,
+                        scale=xsc[b][:, 4 * g + t : 4 * g + t + 1],
+                    )
+                nc.vector.tensor_copy(
+                    out=hg[:].rearrange("q (i p t) -> q i p t", i=4, t=4),
+                    in_=xs[:].rearrange("q t (p i) -> q i p t", i=4),
+                )
+                return
             nc.vector.tensor_tensor(
                 out=hg[:].rearrange("q (i p t) -> q i p t", i=4, t=4),
                 in0=x_sb[:, b, 2 * g : 2 * g + 2, :].rearrange("q u (e p i) -> q i p (u e)", e=2, i=4),
@@ -289,7 +305,7 @@ def tile_axialattentionblock_pa_kernel(
             for i in range(4):
                 for n in range(4):
                     k = 4 * i + n
-                    junk = jp.tile([P, P], F32, name="junk")
+                    junk = jp.tile([P, P], BF16, name="junk")
                     nc.scalar.activation(
                         out=junk[:],
                         in_=S[p]["zs"][i][:, P * n : P * (n + 1)],

@@ -15,7 +15,6 @@ ACT = mybir.ActivationFunctionType
 P = 128
 FLOPS = 2 * 3072 * 1024 * 1024
 MANUAL = False
-N_UNITS = ()
 
 Q0, K0, Q1, K1, V0, V1 = (0, 0), (1, 0), (0, 1), (1, 1), (2, 0), (2, 1)
 LOAD_ORDER = (Q0, K0, Q1, K1, V0, V1)
@@ -31,12 +30,11 @@ def tile_axialattentionblock_pa_kernel(
         const = ctx.enter_context(tc.tile_pool(name="const", bufs=1))
         wgp = ctx.enter_context(tc.tile_pool(name="wgp", bufs=3))
         hgp = ctx.enter_context(tc.tile_pool(name="hgp", bufs=2))
-        xsp = ctx.enter_context(tc.tile_pool(name="xsp", bufs=1))
-        small = ctx.enter_context(tc.tile_pool(name="small", bufs=6))
-        zp = ctx.enter_context(tc.tile_pool(name="zp", bufs=16))
+        small = ctx.enter_context(tc.tile_pool(name="small", bufs=4))
+        zp = ctx.enter_context(tc.tile_pool(name="zp", bufs=12))
         op = ctx.enter_context(tc.tile_pool(name="op", bufs=3))
         vp = ctx.enter_context(tc.tile_pool(name="vp", bufs=2))
-        jp = ctx.enter_context(tc.tile_pool(name="jp", bufs=8))
+        jp = ctx.enter_context(tc.tile_pool(name="jp", bufs=2))
         psc = ctx.enter_context(tc.psum_pool(name="psc", bufs=1))
         psx = ctx.enter_context(tc.psum_pool(name="psx", bufs=4))
         psa = ctx.enter_context(tc.psum_pool(name="psa", bufs=3))
@@ -135,21 +133,6 @@ def tile_axialattentionblock_pa_kernel(
 
         def x_scale(b, g):
             hg = hgp.tile([P, 2048], BF16, name="hg", align_bytes=64)
-            hgs[(b, g)] = hg
-            if (b, g) == (0, 1):
-                xs = xsp.tile([P, 4, 512], BF16, name="xs")
-                for t in range(4):
-                    nc.scalar.activation(
-                        out=xs[:, t, :],
-                        in_=x_sb[:, b, 2 * g + t // 2, 512 * (t % 2) : 512 * (t % 2 + 1)],
-                        func=ACT.Copy,
-                        scale=xsc[b][:, 4 * g + t : 4 * g + t + 1],
-                    )
-                nc.vector.tensor_copy(
-                    out=hg[:].rearrange("q (i p t) -> q i p t", i=4, t=4),
-                    in_=xs[:].rearrange("q t (p i) -> q i p t", i=4),
-                )
-                return
             nc.vector.tensor_tensor(
                 out=hg[:].rearrange("q (i p t) -> q i p t", i=4, t=4),
                 in0=x_sb[:, b, 2 * g : 2 * g + 2, :].rearrange("q u (e p i) -> q i p (u e)", e=2, i=4),
@@ -235,30 +218,20 @@ def tile_axialattentionblock_pa_kernel(
                 )
             store(chunk, b, vst)
 
-        tree = const.tile([P, 8, 2, 64], F32, name="tree")
-        nsb = const.tile([P, 8, 2], F32, name="nsb")
+        sumb = const.tile([P, 16], F32, name="sumb")
+        nsb = const.tile([P, 16], F32, name="nsb")
 
         def bias_sums():
-            nc.gpsimd.tensor_tensor(
-                out=tree[:], in0=b_bc[:, :, 0:2, 0:64], in1=b_bc[:, :, 0:2, 64:128], op=ALU.add
-            )
-            width = 32
-            while width >= 1:
-                nc.gpsimd.tensor_tensor(
-                    out=tree[:, :, :, 0:width],
-                    in0=tree[:, :, :, 0:width],
-                    in1=tree[:, :, :, width : 2 * width],
-                    op=ALU.add,
-                )
-                width = width // 2
-            nc.gpsimd.tensor_scalar(
-                out=nsb[:],
-                in0=tree[:, :, :, 0],
-                scalar1=-1.0 / 128.0,
-                scalar2=0.0,
-                op0=ALU.mult,
-                op1=ALU.add,
-            )
+            for kind in range(2):
+                for n in range(8):
+                    junk = jp.tile([P, P], F32, name="junk")
+                    nc.scalar.activation(
+                        out=junk[:],
+                        in_=b_bc[:, n, kind, :],
+                        func=ACT.Identity,
+                        accum_out=sumb[:, 8 * kind + n : 8 * kind + n + 1],
+                    )
+            nc.vector.tensor_scalar_mul(out=nsb[:], in0=sumb[:], scalar1=-1.0 / 128.0)
 
         S = {}
 
@@ -277,7 +250,8 @@ def tile_axialattentionblock_pa_kernel(
                         func=ACT.Identity,
                         accum_out=su[:, 4 * i + n : 4 * i + n + 1],
                     )
-                nc.gpsimd.tensor_tensor(
+                adder = nc.vector if (b == 1 and i == 3) else nc.gpsimd
+                adder.tensor_tensor(
                     out=z[:].rearrange("q (n c) -> q n c", c=P),
                     in0=z[:].rearrange("q (n c) -> q n c", c=P),
                     in1=bias_of(chunk),
@@ -289,11 +263,12 @@ def tile_axialattentionblock_pa_kernel(
         def stage_n(p):
             (kind, half), b = QK_UNITS[p]
             negm = small.tile([P, 16], F32, name="negm")
+            c0 = 8 * kind + 4 * half
             nc.vector.scalar_tensor_tensor(
                 out=negm[:].rearrange("q (i n) -> q i n", n=4),
                 in0=S[p]["su"][:].rearrange("q (i n) -> q i n", n=4),
                 scalar=-1.0 / 128.0,
-                in1=nsb[:, 4 * half : 4 * half + 4, kind].unsqueeze(1).to_broadcast([P, 4, 4]),
+                in1=nsb[:, c0 : c0 + 4].unsqueeze(1).to_broadcast([P, 4, 4]),
                 op0=ALU.mult,
                 op1=ALU.add,
             )
@@ -305,7 +280,7 @@ def tile_axialattentionblock_pa_kernel(
             for i in range(4):
                 for n in range(4):
                     k = 4 * i + n
-                    junk = jp.tile([P, P], BF16, name="junk")
+                    junk = jp.tile([P, P], F32, name="junk")
                     nc.scalar.activation(
                         out=junk[:],
                         in_=S[p]["zs"][i][:, P * n : P * (n + 1)],
@@ -318,8 +293,6 @@ def tile_axialattentionblock_pa_kernel(
             S[p]["sd"] = sd
 
         def stage_mv(p):
-            if p in N_UNITS:
-                return
             (kind, half), b = QK_UNITS[p]
             negm = S[p]["negm"]
             ost = op.tile([P, 4, 4, P], F32, name="ost")
@@ -339,46 +312,9 @@ def tile_axialattentionblock_pa_kernel(
         def stage_f(p, by_head):
             chunk, b = QK_UNITS[p]
             kind, half = chunk
+            ost = S[p]["ost"]
             rs = small.tile([P, 16], F32, name="rs")
             nc.vector.reciprocal(out=rs[:], in_=S[p]["sd"][:])
-            if p in N_UNITS:
-                nmr = small.tile([P, 16], F32, name="nmr")
-                nc.vector.tensor_tensor(out=nmr[:], in0=S[p]["negm"][:], in1=rs[:], op=ALU.mult)
-                ost = op.tile([P, 4, 4, P], F32, name="ost")
-                gain = lnc[:, P * kind : P * (kind + 1)].unsqueeze(1)
-                shift = lnc[:, 256 + P * kind : 256 + P * (kind + 1)].unsqueeze(1)
-                for n in range(4):
-                    for i in range(4):
-                        k = 4 * i + n
-                        nc.scalar.activation(
-                            out=ost[:, n, i, :],
-                            in_=S[p]["zs"][i][:, P * n : P * (n + 1)],
-                            func=ACT.Identity,
-                            bias=nmr[:, k : k + 1],
-                            scale=rs[:, k : k + 1],
-                        )
-                    if by_head:
-                        nc.vector.tensor_tensor(
-                            out=ost[:, n], in0=ost[:, n], in1=gain.to_broadcast([P, 4, P]), op=ALU.mult
-                        )
-                        nc.vector.tensor_tensor(
-                            out=ost[:, n], in0=ost[:, n], in1=shift.to_broadcast([P, 4, P]), op=ALU.add
-                        )
-                        nc.sync.dma_start(
-                            out=outs[kind][b, 4 * half + n].rearrange("h (w i) c -> (h w) (i c)", i=4),
-                            in_=ost[:, n].rearrange("q i c -> q (i c)"),
-                        )
-                if not by_head:
-                    flat = ost[:].rearrange("q n i c -> q (n i) c")
-                    nc.vector.tensor_tensor(
-                        out=flat, in0=flat, in1=gain.to_broadcast([P, 16, P]), op=ALU.mult
-                    )
-                    nc.vector.tensor_tensor(
-                        out=flat, in0=flat, in1=shift.to_broadcast([P, 16, P]), op=ALU.add
-                    )
-                    store(chunk, b, ost)
-                return
-            ost = S[p]["ost"]
             for n in range(4):
                 for i in range(4):
                     k = 4 * i + n

from contextlib import ExitStack

import concourse.masks as masks
import concourse.mybir as mybir

F32 = mybir.dt.float32
BF16 = mybir.dt.bfloat16
U32 = mybir.dt.uint32
U8 = mybir.dt.uint8
I32 = mybir.dt.int32
FP8X4 = mybir.dt.float8_e4m3fn_x4
ALU = mybir.AluOpType
ACT = mybir.ActivationFunctionType

P = 128
FLOPS = 2 * 3072 * 1024 * 1024
MANUAL = False

Q0, K0, Q1, K1, V0, V1 = (0, 0), (1, 0), (0, 1), (1, 1), (2, 0), (2, 1)
LOAD_ORDER = (Q0, K0, Q1, K1, V0, V1)
QK_UNITS = ((Q0, 0), (K0, 0), (Q1, 0), (K1, 0), (Q0, 1), (K0, 1), (Q1, 1), (K1, 1))


def tile_axialattentionblock_pa_kernel(
    tc, x, norm1_w, qkv_w, qkv_b, qn_w, qn_b, kn_w, kn_b, out_0, out_1, out_2
):
    nc = tc.nc
    outs = (out_0, out_1, out_2)
    with ExitStack() as ctx:
        const = ctx.enter_context(tc.tile_pool(name="const", bufs=1))
        wgp = ctx.enter_context(tc.tile_pool(name="wgp", bufs=3))
        hgp = ctx.enter_context(tc.tile_pool(name="hgp", bufs=2))
        small = ctx.enter_context(tc.tile_pool(name="small", bufs=4))
        zp = ctx.enter_context(tc.tile_pool(name="zp", bufs=12))
        op = ctx.enter_context(tc.tile_pool(name="op", bufs=3))
        vp = ctx.enter_context(tc.tile_pool(name="vp", bufs=2))
        jp = ctx.enter_context(tc.tile_pool(name="jp", bufs=2))
        psc = ctx.enter_context(tc.psum_pool(name="psc", bufs=1))
        psx = ctx.enter_context(tc.psum_pool(name="psx", bufs=4))
        psa = ctx.enter_context(tc.psum_pool(name="psa", bufs=3))
        if MANUAL:
            ctx.enter_context(tc.manual_schedule())

        x_sb = const.tile([P, 2, 4, 1024], BF16, name="x_sb")
        b_bc = const.tile([P, 8, 3, P], BF16, name="b_bc")
        w_view = qkv_w.rearrange("(n t p) k -> t p n k", t=3, p=P)
        wraw = {}

        def load_x(b, g):
            nc.sync.dma_start(
                out=x_sb[:, b, 2 * g : 2 * g + 2, :],
                in_=x[b].rearrange("(r q e) h w -> q r (e h w)", r=4, e=2)[:, 2 * g : 2 * g + 2, :],
            )

        def load_w(chunk):
            kind, half = chunk
            wr = const.tile([P, 4, 1024], BF16, name="wraw%d%d" % chunk)
            nc.sync.dma_start(out=wr[:], in_=w_view[kind, :, 4 * half : 4 * half + 4, :])
            wraw[chunk] = wr

        load_x(0, 0)
        load_x(0, 1)
        load_w(Q0)
        load_w(K0)
        nc.sync.dma_start(
            out=b_bc[:].rearrange("q n t c -> q (n t c)"), in_=qkv_b.partition_broadcast(P)
        )
        load_w(Q1)
        load_w(K1)
        load_x(1, 0)
        load_x(1, 1)
        load_w(V0)
        load_w(V1)

        wrow = const.tile([P, 512], BF16, name="wrow")
        nc.vector.memset(wrow[:].bitcast(I32), 0)
        for k, vec in enumerate((qn_w, kn_w, qn_b, kn_b)):
            nc.scalar.dma_start(
                out=wrow[0:1, P * k : P * (k + 1)], in_=vec.rearrange("(o n) -> o n", o=1)
            )
        nw = const.tile([P, 8], BF16, name="nw")
        with nc.allow_non_contiguous_dma(reason="1024 gains, a pair to a piece"):
            nc.scalar.dma_start(
                out=nw[:].rearrange("q (r e) -> q r e", e=2),
                in_=norm1_w.rearrange("(r q e) -> q r e", r=4, e=2),
            )

        ones = const.tile([P, P], BF16, name="ones")
        nc.vector.memset(ones[:], 1.0)
        one1 = const.tile([P, 1], F32, name="one1")
        nc.vector.memset(one1[:], 1.0)
        eps = const.tile([P, 1], F32, name="eps")
        nc.vector.memset(eps[:], 1e-5)
        warm = const.tile([P, 1], F32, name="warm")
        nc.scalar.activation(out=warm[:], in_=one1[:], func=ACT.Sqrt)
        ident = const.tile([P, P], F32, name="ident")
        masks.make_identity(nc, ident[:])

        lnc = psc.tile([P, 512], F32, name="lnc")
        nc.tensor.matmul(out=lnc[:], lhsT=ones[:], rhs=wrow[:], start=True, stop=True)

        st = const.tile([P, 2, 8, 6], F32, name="st")
        xsc = {}
        hgs = {}
        hc = {}
        hs = {}

        def x_stats(b):
            for s in range(8):
                r, e = divmod(s, 2)
                nc.vector.bn_stats(out=st[:, b, s, :], in_=x_sb[:, b, r, 512 * e : 512 * (e + 1)])

        def x_small(b):
            d = small.tile([P, 8], F32, name="xd")
            nc.vector.tensor_tensor(out=d[:], in0=st[:, b, :, 1], in1=st[:, b, :, 4], op=ALU.subtract)
            d2 = small.tile([P, 8], F32, name="xd2")
            nc.vector.tensor_tensor(out=d2[:], in0=d[:], in1=d[:], op=ALU.mult)
            m2 = small.tile([P, 8], F32, name="xm2")
            nc.vector.tensor_tensor(out=m2[:], in0=st[:, b, :, 2], in1=st[:, b, :, 5], op=ALU.add)
            ss = small.tile([P, 8], F32, name="xss")
            nc.vector.scalar_tensor_tensor(
                out=ss[:], in0=d2[:], scalar=128.0, in1=m2[:], op0=ALU.mult, op1=ALU.add
            )
            sd = small.tile([P, 8], F32, name="xsd")
            nc.scalar.activation(out=sd[:], in_=ss[:], func=ACT.Sqrt, scale=1.0 / 511.0)
            den = small.tile([P, 8], F32, name="xden")
            nc.vector.tensor_scalar_add(out=den[:], in0=sd[:], scalar1=1e-8)
            rec = small.tile([P, 8], F32, name="xrec")
            nc.vector.reciprocal(out=rec[:], in_=den[:])
            sc = small.tile([P, 8], F32, name="xsc")
            nc.vector.tensor_tensor(out=sc[:], in0=rec[:], in1=nw[:], op=ALU.mult)
            xsc[b] = sc

        def x_scale(b, g):
            hg = hgp.tile([P, 2048], BF16, name="hg", align_bytes=64)
            nc.vector.tensor_tensor(
                out=hg[:].rearrange("q (i p t) -> q i p t", i=4, t=4),
                in0=x_sb[:, b, 2 * g : 2 * g + 2, :].rearrange("q u (e p i) -> q i p (u e)", e=2, i=4),
                in1=xsc[b][:, 4 * g : 4 * g + 4].unsqueeze(1).unsqueeze(1).to_broadcast([P, 4, P, 4]),
                op=ALU.mult,
            )
            hgs[(b, g)] = hg

        def x_quant(b, g):
            codes = const.tile([P, 512], U32, name="hc%d%d" % (b, g), align_bytes=64)
            scales = const.tile([P, 512], U8, name="hs%d%d" % (b, g), align_bytes=64)
            nc.vector.quantize_mx(out=codes[:].bitcast(FP8X4), scales=scales[:], in_=hgs[(b, g)][:])
            hc[(b, g)] = codes
            hs[(b, g)] = scales

        wgs = {}
        wc = {}
        ws = {}

        def w_turn(chunk):
            wrf = wraw[chunk][:].bitcast(F32)
            wg = wgp.tile([P, 2, 2048], BF16, name="wg", align_bytes=64)
            wgf = wg[:].bitcast(F32)
            for g in range(2):
                for h in range(2):
                    tp = psx.tile([P, 2, 2, P], F32, tag="aux", name="tp")
                    for u in range(2):
                        for nn in range(2):
                            c0 = P * (2 * g + u)
                            nc.tensor.transpose(
                                out=tp[:, u, nn, :],
                                in_=wrf[:, 2 * h + nn, c0 : c0 + P],
                                identity=ident[:],
                            )
                    nc.scalar.copy(
                        out=wgf[:, g, 512 * h : 512 * (h + 1)].rearrange("q (o u) -> q o u", u=2),
                        in_=tp[:].rearrange("q u n p -> q (n p) u"),
                    )
            wgs[chunk] = wg
            wc[chunk] = const.tile([P, 2, 512], U32, name="wc%d%d" % chunk, align_bytes=64)
            ws[chunk] = const.tile([P, 2, 512], U8, name="ws%d%d" % chunk, align_bytes=64)

        def w_quant(chunk, g):
            nc.vector.quantize_mx(
                out=wc[chunk][:, g, :].bitcast(FP8X4),
                scales=ws[chunk][:, g, :],
                in_=wgs[chunk][:, g, :],
            )

        def product(acc, chunk, b, i):
            for g in range(2):
                nc.tensor.matmul_mx(
                    out=acc[:],
                    lhsT=hc[(b, g)][:, P * i : P * (i + 1)].bitcast(FP8X4),
                    lhsT_scale=hs[(b, g)][:, P * i : P * (i + 1)],
                    rhs=wc[chunk][:, g, :].bitcast(FP8X4),
                    rhs_scale=ws[chunk][:, g, :],
                    start=(g == 0),
                    stop=(g == 1),
                )

        def bias_of(chunk):
            kind, half = chunk
            return b_bc[:, 4 * half : 4 * half + 4, kind, :]

        def store(chunk, b, tile_):
            kind, half = chunk
            nc.sync.dma_start(
                out=outs[kind][b, 4 * half : 4 * half + 4].rearrange("n h (w i) c -> (h w) n (i c)", i=4),
                in_=tile_[:].rearrange("q n i c -> q n (i c)"),
            )

        def v_unit(chunk, b):
            vst = vp.tile([P, 4, 4, P], F32, name="vst")
            for i in range(4):
                acc = psx.tile([P, 512], F32, tag="aux", name="vacc")
                product(acc, chunk, b, i)
                nc.vector.tensor_tensor(
                    out=vst[:, :, i, :],
                    in0=acc[:].rearrange("q (n c) -> q n c", c=P),
                    in1=bias_of(chunk),
                    op=ALU.add,
                )
            store(chunk, b, vst)

        sumb = const.tile([P, 16], F32, name="sumb")
        nsb = const.tile([P, 16], F32, name="nsb")

        def bias_sums():
            for kind in range(2):
                for n in range(8):
                    junk = jp.tile([P, P], F32, name="junk")
                    nc.scalar.activation(
                        out=junk[:],
                        in_=b_bc[:, n, kind, :],
                        func=ACT.Identity,
                        accum_out=sumb[:, 8 * kind + n : 8 * kind + n + 1],
                    )
            nc.vector.tensor_scalar_mul(out=nsb[:], in0=sumb[:], scalar1=-1.0 / 128.0)

        S = {}

        def stage_e(p):
            chunk, b = QK_UNITS[p]
            su = small.tile([P, 16], F32, name="su")
            zs = []
            for i in range(4):
                acc = psa.tile([P, 512], F32, name="acc")
                product(acc, chunk, b, i)
                z = zp.tile([P, 512], F32, name="z")
                for n in range(4):
                    nc.scalar.activation(
                        out=z[:, P * n : P * (n + 1)],
                        in_=acc[:, P * n : P * (n + 1)],
                        func=ACT.Identity,
                        accum_out=su[:, 4 * i + n : 4 * i + n + 1],
                    )
                adder = nc.vector if (b == 1 and i == 3) else nc.gpsimd
                adder.tensor_tensor(
                    out=z[:].rearrange("q (n c) -> q n c", c=P),
                    in0=z[:].rearrange("q (n c) -> q n c", c=P),
                    in1=bias_of(chunk),
                    op=ALU.add,
                )
                zs.append(z)
            S[p] = {"su": su, "zs": zs}

        def stage_n(p):
            (kind, half), b = QK_UNITS[p]
            negm = small.tile([P, 16], F32, name="negm")
            c0 = 8 * kind + 4 * half
            nc.vector.scalar_tensor_tensor(
                out=negm[:].rearrange("q (i n) -> q i n", n=4),
                in0=S[p]["su"][:].rearrange("q (i n) -> q i n", n=4),
                scalar=-1.0 / 128.0,
                in1=nsb[:, c0 : c0 + 4].unsqueeze(1).to_broadcast([P, 4, 4]),
                op0=ALU.mult,
                op1=ALU.add,
            )
            S[p]["negm"] = negm

        def stage_ms(p):
            negm = S[p]["negm"]
            ssq = small.tile([P, 16], F32, name="ssq")
            for i in range(4):
                for n in range(4):
                    k = 4 * i + n
                    junk = jp.tile([P, P], F32, name="junk")
                    nc.scalar.activation(
                        out=junk[:],
                        in_=S[p]["zs"][i][:, P * n : P * (n + 1)],
                        func=ACT.Square,
                        bias=negm[:, k : k + 1],
                        accum_out=ssq[:, k : k + 1],
                    )
            sd = small.tile([P, 16], F32, name="sd")
            nc.scalar.activation(out=sd[:], in_=ssq[:], func=ACT.Sqrt, bias=eps[:], scale=1.0 / 128.0)
            S[p]["sd"] = sd

        def stage_mv(p):
            (kind, half), b = QK_UNITS[p]
            negm = S[p]["negm"]
            ost = op.tile([P, 4, 4, P], F32, name="ost")
            for i in range(4):
                for n in range(4):
                    k = 4 * i + n
                    nc.vector.scalar_tensor_tensor(
                        out=ost[:, n, i, :],
                        in0=S[p]["zs"][i][:, P * n : P * (n + 1)],
                        scalar=negm[:, k : k + 1],
                        in1=lnc[:, P * kind : P * (kind + 1)],
                        op0=ALU.add,
                        op1=ALU.mult,
                    )
            S[p]["ost"] = ost

        def stage_f(p, by_head):
            chunk, b = QK_UNITS[p]
            kind, half = chunk
            ost = S[p]["ost"]
            rs = small.tile([P, 16], F32, name="rs")
            nc.vector.reciprocal(out=rs[:], in_=S[p]["sd"][:])
            for n in range(4):
                for i in range(4):
                    k = 4 * i + n
                    nc.vector.scalar_tensor_tensor(
                        out=ost[:, n, i, :],
                        in0=ost[:, n, i, :],
                        scalar=rs[:, k : k + 1],
                        in1=lnc[:, 256 + P * kind : 256 + P * (kind + 1)],
                        op0=ALU.mult,
                        op1=ALU.add,
                    )
                if by_head:
                    nc.sync.dma_start(
                        out=outs[kind][b, 4 * half + n].rearrange("h (w i) c -> (h w) (i c)", i=4),
                        in_=ost[:, n].rearrange("q i c -> q (i c)"),
                    )
            if not by_head:
                store(chunk, b, ost)

        x_stats(0)
        x_small(0)
        w_turn(Q0)
        x_scale(0, 0)
        w_quant(Q0, 0)
        x_quant(0, 0)
        x_scale(0, 1)
        w_quant(Q0, 1)
        x_quant(0, 1)
        w_turn(K0)
        bias_sums()
        w_quant(K0, 0)
        w_quant(K0, 1)
        w_turn(Q1)

        def filler(p):
            if p == 0:
                w_turn(K1)
                w_quant(Q1, 0)
                w_quant(Q1, 1)
                x_stats(1)
                x_small(1)
            elif p == 1:
                w_turn(V0)
                x_scale(1, 0)
                w_quant(K1, 0)
                w_quant(K1, 1)
                x_quant(1, 0)
            elif p == 2:
                w_turn(V1)
                x_scale(1, 1)
                w_quant(V0, 0)
                w_quant(V0, 1)
                x_quant(1, 1)
            elif p == 3:
                w_quant(V1, 0)
                w_quant(V1, 1)
                v_unit(V0, 0)
            elif p == 4:
                v_unit(V1, 0)
            elif p == 5:
                v_unit(V0, 1)
            elif p == 6:
                v_unit(V1, 1)

        for p in range(10):
            if p < 8:
                stage_e(p)
            if 0 <= p - 2 < 8:
                stage_f(p - 2, p - 2 == 7)
            if 0 <= p - 1 < 8:
                stage_mv(p - 1)
                stage_ms(p - 1)
            if p < 8:
                stage_n(p)
            filler(p)
